import numpy as np
import ml_dtypes


def mxq(x, axis, fmt="e4m3"):
    dtype, down = {"e4m3": (ml_dtypes.float8_e4m3fn, 7), "e5m2": (ml_dtypes.float8_e5m2, 14)}[fmt]
    v = np.moveaxis(np.asarray(x, np.float32).astype(ml_dtypes.bfloat16).astype(np.float64), axis, -1)
    blocks = v.reshape(v.shape[:-1] + (-1, 32))
    amax = np.abs(blocks).max(-1, keepdims=True)
    byte = np.maximum(np.where(amax > 0, np.frexp(amax)[1] - 1 + 127, 0) - down, 1)
    scale = np.exp2(byte - 127.0)
    codes = (blocks / scale).astype(np.float32).astype(dtype).astype(np.float64)
    return np.moveaxis((codes * scale).reshape(v.shape), -1, axis)


WIDE = False


def mx_kscale(k):
    if not WIDE:
        return np.ones(k)
    levels = np.array([20, -20, 10, -10, 0])
    a = np.random.permutation(np.resize(levels, k // 512 * 4)).reshape(k // 512, 4)
    idx = np.arange(k)
    return np.exp2(a[idx // 512, idx % 128 // 32])


BF16 = ml_dtypes.bfloat16


def bf(x):
    return np.asarray(x, np.float32).astype(BF16)


def f64(x):
    return np.asarray(x).astype(np.float64)


N_TOK, IN_F, OUT_F, N_BITS = 2048, 1024, 512, 8
STEP_SIZE = 0.0078125
W_STD = np.sqrt((4.0 ** N_BITS - 1.0) / 36.0) * STEP_SIZE


def setup_inputs():
    s = mx_kscale(N_TOK)[:, None]
    x = np.random.standard_normal((N_TOK, IN_F)) * (2.0 / (W_STD * np.sqrt(IN_F))) * s
    w_twos = np.random.uniform(0.0, 1.0, (OUT_F, IN_F, N_BITS))
    b = np.random.standard_normal(OUT_F)
    base_vals = np.array([2.0 ** i for i in range(N_BITS - 1, -1, -1)])
    base_vals[0] = -base_vals[0]
    g = np.random.standard_normal((N_TOK, OUT_F)) * np.exp2(np.random.randint(-12, 1, (N_TOK, 1))) * 8.0 / s
    return {"x": bf(x), "w_twos": bf(w_twos), "b": bf(b), "base": bf(base_vals.reshape(1, 1, N_BITS)), "grad_out": bf(g)}


def reference(x, w_twos, b, base, grad_out):
    gw = mxq(f64(grad_out), 0, "e5m2").T @ mxq(f64(x), 0, "e4m3")
    return gw[:, :, None] * f64(base) * STEP_SIZE

@@ -1,0 +1,148 @@
+from contextlib import ExitStack
+
+import concourse.mybir as mybir
+
+F32 = mybir.dt.float32
+BF16 = mybir.dt.bfloat16
+U32 = mybir.dt.uint32
+U8 = mybir.dt.uint8
+E4M3X4 = mybir.dt.float8_e4m3fn_x4
+E5M2X4 = mybir.dt.float8_e5m2_x4
+MULT = mybir.AluOpType.mult
+
+P = 128
+PACK = 4
+K_PASS = P * PACK
+N_TOK, IN_F, OUT_F, N_BITS = 2048, 1024, 512, 8
+STEP_SIZE = 0.0078125
+PASSES = N_TOK // K_PASS
+N_TILE = 512
+M_TILES = OUT_F // P
+N_TILES = IN_F // N_TILE
+PIECE = 256
+GPSIMD_M = 1
+VECTOR_M = (0, 2, 3)
+
+FLOPS = 2 * N_TOK * IN_F * OUT_F
+BYTES = 2 * N_TOK * (IN_F + OUT_F) + 2 * N_BITS + 4 * OUT_F * IN_F * N_BITS
+
+
+def tile_auglag_kernel(tc, x, w_twos, b, base, grad_out, out):
+    nc = tc.nc
+    with ExitStack() as ctx:
+        raw = ctx.enter_context(tc.tile_pool(name="raw", bufs=1))
+        keep = ctx.enter_context(tc.tile_pool(name="keep", bufs=1))
+        grp = ctx.enter_context(tc.tile_pool(name="grp", bufs=4))
+        vout = ctx.enter_context(tc.tile_pool(name="vout", bufs=8))
+        gout = ctx.enter_context(tc.tile_pool(name="gout", bufs=4))
+        gsum = ctx.enter_context(tc.tile_pool(name="gsum", bufs=2))
+        psum = ctx.enter_context(tc.psum_pool(name="acc", bufs=1))
+        ctx.enter_context(tc.manual_schedule())
+
+        g_codes = keep.tile([P, PASSES, OUT_F], U32, align_bytes=64)
+        g_scales = keep.tile([P, PASSES, OUT_F], U8, align_bytes=64)
+        x_codes = keep.tile([P, PASSES, IN_F], U32, align_bytes=64)
+        x_scales = keep.tile([P, PASSES, IN_F], U8, align_bytes=64)
+        base_bf = keep.tile([P, N_BITS], BF16)
+        table = keep.tile([P, N_BITS], F32)
+
+        nc.scalar.dma_start(out=base_bf[:], in_=base.rearrange("a b k -> (a b k)").partition_broadcast(P))
+        nc.gpsimd.tensor_scalar_mul(out=table[:], in0=base_bf[:], scalar1=STEP_SIZE)
+
+        def load(src, name):
+            t = raw.tile([P, PACK, N_TILE], BF16, name=name)
+            nc.sync.dma_start(out=t[:], in_=src.rearrange("(p j) w -> p j w", j=PACK))
+            return t
+
+        g_raw = []
+        x_raw = [[], []]
+        for c in range(PASSES):
+            g_raw.append(load(grad_out[c * K_PASS : (c + 1) * K_PASS, :], "graw%d" % c))
+            x_raw[0].append(load(x[c * K_PASS : (c + 1) * K_PASS, 0:N_TILE], "xraw0%d" % c))
+        for c in range(PASSES):
+            x_raw[1].append(load(x[c * K_PASS : (c + 1) * K_PASS, N_TILE : 2 * N_TILE], "xraw1%d" % c))
+
+        def regroup(copy, src, tag, name):
+            t = grp.tile([P, N_TILE, PACK], BF16, name=name, tag=tag, align_bytes=64)
+            copy(
+                out=t[:].rearrange("p (c i) t -> p c t i", i=4),
+                in_=src[:].rearrange("p t (c i) -> p c t i", i=4),
+            )
+            return t
+
+        def quantise(grouped, codes, scales, fmt):
+            nc.vector.quantize_mx(
+                out=codes.bitcast(fmt), scales=scales, in_=grouped[:].rearrange("p w t -> p (w t)")
+            )
+
+        acc = [
+            [psum.tile([P, N_TILE], F32, name="acc%d%d" % (m, n)) for n in range(N_TILES)]
+            for m in range(M_TILES)
+        ]
+
+        def passes(c, n):
+            for m in range(M_TILES):
+                nc.tensor.matmul_mx(
+                    out=acc[m][n][:],
+                    lhsT=g_codes[:, c, m * P : (m + 1) * P].bitcast(E5M2X4),
+                    lhsT_scale=g_scales[:, c, m * P : (m + 1) * P],
+                    rhs=x_codes[:, c, n * N_TILE : (n + 1) * N_TILE].bitcast(E4M3X4),
+                    rhs_scale=x_scales[:, c, n * N_TILE : (n + 1) * N_TILE],
+                    start=(c == 0),
+                    stop=(c == PASSES - 1),
+                )
+
+        def spread(engine, queue, pool, sums, m, n, h):
+            t = pool.tile([P, PIECE, N_BITS], F32, name="spread")
+            engine.tensor_tensor(
+                out=t[:],
+                in0=sums[:, h * PIECE : (h + 1) * PIECE].unsqueeze(2).to_broadcast([P, PIECE, N_BITS]),
+                in1=table[:].unsqueeze(1).to_broadcast([P, PIECE, N_BITS]),
+                op=MULT,
+            )
+            i0 = n * N_TILE + h * PIECE
+            queue.dma_start(out=out[m * P : (m + 1) * P, i0 : i0 + PIECE, :], in_=t[:])
+
+        def vector_spread(m, n, h):
+            spread(nc.vector, nc.sync, vout, acc[m][n], m, n, h)
+
+        def gpsimd_bank(n):
+            sums = gsum.tile([P, N_TILE], F32, name="sums")
+            nc.scalar.copy(out=sums[:], in_=acc[GPSIMD_M][n][:])
+            for h in range(N_TILE // PIECE):
+                spread(nc.gpsimd, nc.gpsimd, gout, sums, GPSIMD_M, n, h)
+
+        def quantise_x(grouped, c, n):
+            cols = slice(n * N_TILE, (n + 1) * N_TILE)
+            quantise(grouped, x_codes[:, c, cols], x_scales[:, c, cols], E4M3X4)
+
+        for c in range(PASSES):
+            gg = regroup(nc.scalar.copy, g_raw[c], "byscalar", "gg%d" % c)
+            gx = regroup(nc.vector.tensor_copy, x_raw[0][c], "byvector", "gx%d" % c)
+            quantise(gg, g_codes[:, c, :], g_scales[:, c, :], E5M2X4)
+            quantise_x(gx, c, 0)
+            passes(c, 0)
+
+        late = [regroup(nc.scalar.copy, x_raw[1][0], "byscalar", "gl0")]
+        gpsimd_bank(0)
+        for c in range(1, PASSES):
+            late.append(regroup(nc.scalar.copy, x_raw[1][c], "byscalar", "gl%d" % c))
+
+        vector_spread(0, 0, 0)
+        vector_spread(0, 0, 1)
+        quantise_x(late[0], 0, 1)
+        passes(0, 1)
+        quantise_x(late[1], 1, 1)
+        passes(1, 1)
+        vector_spread(2, 0, 0)
+        quantise_x(late[2], 2, 1)
+        passes(2, 1)
+        vector_spread(2, 0, 1)
+        quantise_x(late[3], 3, 1)
+        passes(3, 1)
+        gpsimd_bank(1)
+        vector_spread(3, 0, 0)
+        vector_spread(3, 0, 1)
+        for m in VECTOR_M:
+            vector_spread(m, 1, 0)
+            vector_spread(m, 1, 1)

@@ -20,6 +20,7 @@ N_TILE = 512
 M_TILES = OUT_F // P
 N_TILES = IN_F // N_TILE
 PIECE = 256
+FIRST_PIECE = 128
 GPSIMD_M = 1
 VECTOR_M = (0, 2, 3)
 
@@ -36,6 +37,7 @@ def tile_auglag_kernel(tc, x, w_twos, b, base, grad_out, out):
         vout = ctx.enter_context(tc.tile_pool(name="vout", bufs=8))
         gout = ctx.enter_context(tc.tile_pool(name="gout", bufs=4))
         gsum = ctx.enter_context(tc.tile_pool(name="gsum", bufs=2))
+        vfirst = ctx.enter_context(tc.tile_pool(name="vfirst", bufs=4))
         psum = ctx.enter_context(tc.psum_pool(name="acc", bufs=1))
         ctx.enter_context(tc.manual_schedule())
 
@@ -92,16 +94,16 @@ def tile_auglag_kernel(tc, x, w_twos, b, base, grad_out, out):
                     stop=(c == PASSES - 1),
                 )
 
-        def spread(engine, queue, pool, sums, m, n, h):
-            t = pool.tile([P, PIECE, N_BITS], F32, name="spread")
+        def spread(engine, queue, pool, sums, m, n, h, width=PIECE):
+            t = pool.tile([P, width, N_BITS], F32, name="spread")
             engine.tensor_tensor(
                 out=t[:],
-                in0=sums[:, h * PIECE : (h + 1) * PIECE].unsqueeze(2).to_broadcast([P, PIECE, N_BITS]),
-                in1=table[:].unsqueeze(1).to_broadcast([P, PIECE, N_BITS]),
+                in0=sums[:, h * width : (h + 1) * width].unsqueeze(2).to_broadcast([P, width, N_BITS]),
+                in1=table[:].unsqueeze(1).to_broadcast([P, width, N_BITS]),
                 op=MULT,
             )
-            i0 = n * N_TILE + h * PIECE
-            queue.dma_start(out=out[m * P : (m + 1) * P, i0 : i0 + PIECE, :], in_=t[:])
+            i0 = n * N_TILE + h * width
+            queue.dma_start(out=out[m * P : (m + 1) * P, i0 : i0 + width, :], in_=t[:])
 
         def vector_spread(m, n, h):
             spread(nc.vector, nc.sync, vout, acc[m][n], m, n, h)
@@ -123,23 +125,16 @@ def tile_auglag_kernel(tc, x, w_twos, b, base, grad_out, out):
             quantise_x(gx, c, 0)
             passes(c, 0)
 
-        late = [regroup(nc.scalar.copy, x_raw[1][0], "byscalar", "gl0")]
         gpsimd_bank(0)
-        for c in range(1, PASSES):
-            late.append(regroup(nc.scalar.copy, x_raw[1][c], "byscalar", "gl%d" % c))
+        late = [regroup(nc.scalar.copy, x_raw[1][c], "byscalar", "gl%d" % c) for c in range(PASSES)]
 
-        vector_spread(0, 0, 0)
-        vector_spread(0, 0, 1)
-        quantise_x(late[0], 0, 1)
-        passes(0, 1)
-        quantise_x(late[1], 1, 1)
-        passes(1, 1)
+        for h in range(N_TILE // FIRST_PIECE):
+            spread(nc.vector, nc.sync, vfirst, acc[0][0], 0, 0, h, FIRST_PIECE)
         vector_spread(2, 0, 0)
-        quantise_x(late[2], 2, 1)
-        passes(2, 1)
         vector_spread(2, 0, 1)
-        quantise_x(late[3], 3, 1)
-        passes(3, 1)
+        for c in range(PASSES):
+            quantise_x(late[c], c, 1)
+            passes(c, 1)
         gpsimd_bank(1)
         vector_spread(3, 0, 0)
         vector_spread(3, 0, 1)

@@ -21,6 +21,7 @@ M_TILES = OUT_F // P
 N_TILES = IN_F // N_TILE
 PIECE = 256
 FIRST_PIECE = 128
+PAD_N = 32
 GPSIMD_M = 1
 VECTOR_M = (0, 2, 3)
 
@@ -45,11 +46,13 @@ def tile_auglag_kernel(tc, x, w_twos, b, base, grad_out, out):
         g_scales = keep.tile([P, PASSES, OUT_F], U8, align_bytes=64)
         x_codes = keep.tile([P, PASSES, IN_F], U32, align_bytes=64)
         x_scales = keep.tile([P, PASSES, IN_F], U8, align_bytes=64)
-        base_bf = keep.tile([P, N_BITS], BF16)
+        base_row = keep.tile([P, PAD_N], BF16)
+        step_mat = keep.tile([P, P], BF16)
         table = keep.tile([P, N_BITS], F32)
 
-        nc.scalar.dma_start(out=base_bf[:], in_=base.rearrange("a b k -> (a b k)").partition_broadcast(P))
-        nc.gpsimd.tensor_scalar_mul(out=table[:], in0=base_bf[:], scalar1=STEP_SIZE)
+        nc.vector.memset(base_row[:], 0.0)
+        nc.gpsimd.memset(step_mat[:], STEP_SIZE)
+        nc.scalar.dma_start(out=base_row[0:1, 0:N_BITS], in_=base.rearrange("a b k -> (a b) k"))
 
         def load(src, name):
             t = raw.tile([P, PACK, N_TILE], BF16, name=name)
@@ -124,6 +127,9 @@ def tile_auglag_kernel(tc, x, w_twos, b, base, grad_out, out):
             quantise(gg, g_codes[:, c, :], g_scales[:, c, :], E5M2X4)
             quantise_x(gx, c, 0)
             passes(c, 0)
+            if c == 1:
+                nc.tensor.matmul(out=acc[3][1][:, 0:PAD_N], lhsT=step_mat[:], rhs=base_row[:], start=True, stop=True)
+        nc.scalar.copy(out=table[:], in_=acc[3][1][:, 0:N_BITS])
 
         gpsimd_bank(0)
         late = [regroup(nc.scalar.copy, x_raw[1][c], "byscalar", "gl%d" % c) for c in range(PASSES)]

@@ -22,8 +22,7 @@ N_TILES = IN_F // N_TILE
 PIECE = 256
 FIRST_PIECE = 128
 PAD_N = 32
-GPSIMD_M = 1
-VECTOR_M = (0, 2, 3)
+TAPER = (32, 32, 64, 128, 256)
 
 FLOPS = 2 * N_TOK * IN_F * OUT_F
 BYTES = 2 * N_TOK * (IN_F + OUT_F) + 2 * N_BITS + 4 * OUT_F * IN_F * N_BITS
@@ -76,17 +75,18 @@ def tile_auglag_kernel(tc, x, w_twos, b, base, grad_out, out):
             return t
 
         def quantise(grouped, codes, scales, fmt):
-            nc.vector.quantize_mx(
-                out=codes.bitcast(fmt), scales=scales, in_=grouped[:].rearrange("p w t -> p (w t)")
-            )
+            nc.vector.quantize_mx(out=codes.bitcast(fmt), scales=scales, in_=grouped.rearrange("p w t -> p (w t)"))
+
+        def quantise_g(grouped, c, lo, hi):
+            quantise(grouped[:, lo:hi, :], g_codes[:, c, lo:hi], g_scales[:, c, lo:hi], E5M2X4)
 
         acc = [
             [psum.tile([P, N_TILE], F32, name="acc%d%d" % (m, n)) for n in range(N_TILES)]
             for m in range(M_TILES)
         ]
 
-        def passes(c, n):
-            for m in range(M_TILES):
+        def passes(c, n, tiles=(0, 1, 2, 3)):
+            for m in tiles:
                 nc.tensor.matmul_mx(
                     out=acc[m][n][:],
                     lhsT=g_codes[:, c, m * P : (m + 1) * P].bitcast(E5M2X4),
@@ -97,53 +97,64 @@ def tile_auglag_kernel(tc, x, w_twos, b, base, grad_out, out):
                     stop=(c == PASSES - 1),
                 )
 
-        def spread(engine, queue, pool, sums, m, n, h, width=PIECE):
+        def spread(engine, queue, pool, sums, m, n, lo, width):
             t = pool.tile([P, width, N_BITS], F32, name="spread")
             engine.tensor_tensor(
                 out=t[:],
-                in0=sums[:, h * width : (h + 1) * width].unsqueeze(2).to_broadcast([P, width, N_BITS]),
+                in0=sums[:, lo : lo + width].unsqueeze(2).to_broadcast([P, width, N_BITS]),
                 in1=table[:].unsqueeze(1).to_broadcast([P, width, N_BITS]),
                 op=MULT,
             )
-            i0 = n * N_TILE + h * width
+            i0 = n * N_TILE + lo
             queue.dma_start(out=out[m * P : (m + 1) * P, i0 : i0 + width, :], in_=t[:])
 
-        def vector_spread(m, n, h):
-            spread(nc.vector, nc.sync, vout, acc[m][n], m, n, h)
+        def vector_bank(m, n):
+            for lo in range(0, N_TILE, PIECE):
+                spread(nc.vector, nc.sync, vout, acc[m][n], m, n, lo, PIECE)
 
-        def gpsimd_bank(n):
+        def copy_sums(m, n):
             sums = gsum.tile([P, N_TILE], F32, name="sums")
-            nc.scalar.copy(out=sums[:], in_=acc[GPSIMD_M][n][:])
-            for h in range(N_TILE // PIECE):
-                spread(nc.gpsimd, nc.gpsimd, gout, sums, GPSIMD_M, n, h)
+            nc.scalar.copy(out=sums[:], in_=acc[m][n][:])
+            return sums
+
+        def gpsimd_bank(sums, m, n, width):
+            for lo in range(0, N_TILE, width):
+                spread(nc.gpsimd, nc.gpsimd, gout, sums, m, n, lo, width)
 
         def quantise_x(grouped, c, n):
             cols = slice(n * N_TILE, (n + 1) * N_TILE)
-            quantise(grouped, x_codes[:, c, cols], x_scales[:, c, cols], E4M3X4)
+            quantise(grouped[:], x_codes[:, c, cols], x_scales[:, c, cols], E4M3X4)
 
         for c in range(PASSES):
             gg = regroup(nc.scalar.copy, g_raw[c], "byscalar", "gg%d" % c)
             gx = regroup(nc.vector.tensor_copy, x_raw[0][c], "byvector", "gx%d" % c)
-            quantise(gg, g_codes[:, c, :], g_scales[:, c, :], E5M2X4)
-            quantise_x(gx, c, 0)
-            passes(c, 0)
+            if c < PASSES - 1:
+                quantise_g(gg, c, 0, OUT_F)
+                quantise_x(gx, c, 0)
+                passes(c, 0)
+            else:
+                quantise_g(gg, c, 0, P)
+                quantise_x(gx, c, 0)
+                passes(c, 0, (0,))
+                quantise_g(gg, c, P, 2 * P)
+                passes(c, 0, (1,))
+                quantise_g(gg, c, 2 * P, 4 * P)
+                passes(c, 0, (2, 3))
             if c == 1:
                 nc.tensor.matmul(out=acc[3][1][:, 0:PAD_N], lhsT=step_mat[:], rhs=base_row[:], start=True, stop=True)
         nc.scalar.copy(out=table[:], in_=acc[3][1][:, 0:N_BITS])
 
-        gpsimd_bank(0)
+        gpsimd_bank(copy_sums(1, 0), 1, 0, FIRST_PIECE)
         late = [regroup(nc.scalar.copy, x_raw[1][c], "byscalar", "gl%d" % c) for c in range(PASSES)]
+        gpsimd_bank(copy_sums(3, 0), 3, 0, PIECE)
 
-        for h in range(N_TILE // FIRST_PIECE):
-            spread(nc.vector, nc.sync, vfirst, acc[0][0], 0, 0, h, FIRST_PIECE)
-        vector_spread(2, 0, 0)
-        vector_spread(2, 0, 1)
+        lo = 0
+        for width in TAPER:
+            spread(nc.vector, nc.sync, vfirst if width <= FIRST_PIECE else vout, acc[0][0], 0, 0, lo, width)
+            lo += width
+        vector_bank(2, 0)
         for c in range(PASSES):
             quantise_x(late[c], c, 1)
             passes(c, 1)
-        gpsimd_bank(1)
-        vector_spread(3, 0, 0)
-        vector_spread(3, 0, 1)
-        for m in VECTOR_M:
-            vector_spread(m, 1, 0)
-            vector_spread(m, 1, 1)
+        for m in range(M_TILES):
+            vector_bank(m, 1)

@@ -22,7 +22,7 @@ N_TILES = IN_F // N_TILE
 PIECE = 256
 FIRST_PIECE = 128
 PAD_N = 32
-TAPER = (32, 32, 64, 128, 256)
+GPSIMD_M = 1
 
 FLOPS = 2 * N_TOK * IN_F * OUT_F
 BYTES = 2 * N_TOK * (IN_F + OUT_F) + 2 * N_BITS + 4 * OUT_F * IN_F * N_BITS
@@ -34,9 +34,9 @@ def tile_auglag_kernel(tc, x, w_twos, b, base, grad_out, out):
         raw = ctx.enter_context(tc.tile_pool(name="raw", bufs=1))
         keep = ctx.enter_context(tc.tile_pool(name="keep", bufs=1))
         grp = ctx.enter_context(tc.tile_pool(name="grp", bufs=4))
-        vout = ctx.enter_context(tc.tile_pool(name="vout", bufs=8))
-        gout = ctx.enter_context(tc.tile_pool(name="gout", bufs=4))
-        gsum = ctx.enter_context(tc.tile_pool(name="gsum", bufs=2))
+        vout = ctx.enter_context(tc.tile_pool(name="vout", bufs=10))
+        gout = ctx.enter_context(tc.tile_pool(name="gout", bufs=2))
+        gsum = ctx.enter_context(tc.tile_pool(name="gsum", bufs=1))
         vfirst = ctx.enter_context(tc.tile_pool(name="vfirst", bufs=4))
         psum = ctx.enter_context(tc.psum_pool(name="acc", bufs=1))
         ctx.enter_context(tc.manual_schedule())
@@ -75,18 +75,17 @@ def tile_auglag_kernel(tc, x, w_twos, b, base, grad_out, out):
             return t
 
         def quantise(grouped, codes, scales, fmt):
-            nc.vector.quantize_mx(out=codes.bitcast(fmt), scales=scales, in_=grouped.rearrange("p w t -> p (w t)"))
-
-        def quantise_g(grouped, c, lo, hi):
-            quantise(grouped[:, lo:hi, :], g_codes[:, c, lo:hi], g_scales[:, c, lo:hi], E5M2X4)
+            nc.vector.quantize_mx(
+                out=codes.bitcast(fmt), scales=scales, in_=grouped[:].rearrange("p w t -> p (w t)")
+            )
 
         acc = [
             [psum.tile([P, N_TILE], F32, name="acc%d%d" % (m, n)) for n in range(N_TILES)]
             for m in range(M_TILES)
         ]
 
-        def passes(c, n, tiles=(0, 1, 2, 3)):
-            for m in tiles:
+        def passes(c, n):
+            for m in range(M_TILES):
                 nc.tensor.matmul_mx(
                     out=acc[m][n][:],
                     lhsT=g_codes[:, c, m * P : (m + 1) * P].bitcast(E5M2X4),
@@ -97,64 +96,52 @@ def tile_auglag_kernel(tc, x, w_twos, b, base, grad_out, out):
                     stop=(c == PASSES - 1),
                 )
 
-        def spread(engine, queue, pool, sums, m, n, lo, width):
+        def spread(engine, queue, pool, sums, m, n, h, width=PIECE):
             t = pool.tile([P, width, N_BITS], F32, name="spread")
             engine.tensor_tensor(
                 out=t[:],
-                in0=sums[:, lo : lo + width].unsqueeze(2).to_broadcast([P, width, N_BITS]),
+                in0=sums[:, h * width : (h + 1) * width].unsqueeze(2).to_broadcast([P, width, N_BITS]),
                 in1=table[:].unsqueeze(1).to_broadcast([P, width, N_BITS]),
                 op=MULT,
             )
-            i0 = n * N_TILE + lo
+            i0 = n * N_TILE + h * width
             queue.dma_start(out=out[m * P : (m + 1) * P, i0 : i0 + width, :], in_=t[:])
 
-        def vector_bank(m, n):
-            for lo in range(0, N_TILE, PIECE):
-                spread(nc.vector, nc.sync, vout, acc[m][n], m, n, lo, PIECE)
+        def vector_spread(m, n, h):
+            spread(nc.vector, nc.sync, vout, acc[m][n], m, n, h)
 
-        def copy_sums(m, n):
+        def gpsimd_bank(n):
             sums = gsum.tile([P, N_TILE], F32, name="sums")
-            nc.scalar.copy(out=sums[:], in_=acc[m][n][:])
-            return sums
-
-        def gpsimd_bank(sums, m, n, width):
-            for lo in range(0, N_TILE, width):
-                spread(nc.gpsimd, nc.gpsimd, gout, sums, m, n, lo, width)
+            nc.scalar.copy(out=sums[:], in_=acc[GPSIMD_M][n][:])
+            for h in range(N_TILE // PIECE):
+                spread(nc.gpsimd, nc.gpsimd, gout, sums, GPSIMD_M, n, h)
 
         def quantise_x(grouped, c, n):
             cols = slice(n * N_TILE, (n + 1) * N_TILE)
-            quantise(grouped[:], x_codes[:, c, cols], x_scales[:, c, cols], E4M3X4)
+            quantise(grouped, x_codes[:, c, cols], x_scales[:, c, cols], E4M3X4)
 
         for c in range(PASSES):
             gg = regroup(nc.scalar.copy, g_raw[c], "byscalar", "gg%d" % c)
             gx = regroup(nc.vector.tensor_copy, x_raw[0][c], "byvector", "gx%d" % c)
-            if c < PASSES - 1:
-                quantise_g(gg, c, 0, OUT_F)
-                quantise_x(gx, c, 0)
-                passes(c, 0)
-            else:
-                quantise_g(gg, c, 0, P)
-                quantise_x(gx, c, 0)
-                passes(c, 0, (0,))
-                quantise_g(gg, c, P, 2 * P)
-                passes(c, 0, (1,))
-                quantise_g(gg, c, 2 * P, 4 * P)
-                passes(c, 0, (2, 3))
+            quantise(gg, g_codes[:, c, :], g_scales[:, c, :], E5M2X4)
+            quantise_x(gx, c, 0)
+            passes(c, 0)
             if c == 1:
                 nc.tensor.matmul(out=acc[3][1][:, 0:PAD_N], lhsT=step_mat[:], rhs=base_row[:], start=True, stop=True)
         nc.scalar.copy(out=table[:], in_=acc[3][1][:, 0:N_BITS])
 
-        gpsimd_bank(copy_sums(1, 0), 1, 0, FIRST_PIECE)
+        gpsimd_bank(0)
         late = [regroup(nc.scalar.copy, x_raw[1][c], "byscalar", "gl%d" % c) for c in range(PASSES)]
-        gpsimd_bank(copy_sums(3, 0), 3, 0, PIECE)
 
-        lo = 0
-        for width in TAPER:
-            spread(nc.vector, nc.sync, vfirst if width <= FIRST_PIECE else vout, acc[0][0], 0, 0, lo, width)
-            lo += width
-        vector_bank(2, 0)
+        for h in range(N_TILE // FIRST_PIECE):
+            spread(nc.vector, nc.sync, vfirst, acc[0][0], 0, 0, h, FIRST_PIECE)
+        vector_spread(2, 0, 0)
+        vector_spread(2, 0, 1)
         for c in range(PASSES):
             quantise_x(late[c], c, 1)
             passes(c, 1)
+        vector_spread(3, 0, 0)
+        vector_spread(3, 0, 1)
         for m in range(M_TILES):
-            vector_bank(m, 1)
+            vector_spread(m, 1, 0)
+            vector_spread(m, 1, 1)

@@ -22,7 +22,6 @@ N_TILES = IN_F // N_TILE
 PIECE = 256
 FIRST_PIECE = 128
 PAD_N = 32
-GPSIMD_M = 1
 
 FLOPS = 2 * N_TOK * IN_F * OUT_F
 BYTES = 2 * N_TOK * (IN_F + OUT_F) + 2 * N_BITS + 4 * OUT_F * IN_F * N_BITS
@@ -36,7 +35,7 @@ def tile_auglag_kernel(tc, x, w_twos, b, base, grad_out, out):
         grp = ctx.enter_context(tc.tile_pool(name="grp", bufs=4))
         vout = ctx.enter_context(tc.tile_pool(name="vout", bufs=10))
         gout = ctx.enter_context(tc.tile_pool(name="gout", bufs=2))
-        gsum = ctx.enter_context(tc.tile_pool(name="gsum", bufs=1))
+        gsum = ctx.enter_context(tc.tile_pool(name="gsum", bufs=2))
         vfirst = ctx.enter_context(tc.tile_pool(name="vfirst", bufs=4))
         psum = ctx.enter_context(tc.psum_pool(name="acc", bufs=1))
         ctx.enter_context(tc.manual_schedule())
@@ -110,11 +109,11 @@ def tile_auglag_kernel(tc, x, w_twos, b, base, grad_out, out):
         def vector_spread(m, n, h):
             spread(nc.vector, nc.sync, vout, acc[m][n], m, n, h)
 
-        def gpsimd_bank(n):
+        def gpsimd_piece(m, n, h):
             sums = gsum.tile([P, N_TILE], F32, name="sums")
-            nc.scalar.copy(out=sums[:], in_=acc[GPSIMD_M][n][:])
-            for h in range(N_TILE // PIECE):
-                spread(nc.gpsimd, nc.gpsimd, gout, sums, GPSIMD_M, n, h)
+            cols = slice(h * PIECE, (h + 1) * PIECE)
+            nc.scalar.copy(out=sums[:, cols], in_=acc[m][n][:, cols])
+            spread(nc.gpsimd, nc.gpsimd, gout, sums, m, n, h)
 
         def quantise_x(grouped, c, n):
             cols = slice(n * N_TILE, (n + 1) * N_TILE)
@@ -130,18 +129,21 @@ def tile_auglag_kernel(tc, x, w_twos, b, base, grad_out, out):
                 nc.tensor.matmul(out=acc[3][1][:, 0:PAD_N], lhsT=step_mat[:], rhs=base_row[:], start=True, stop=True)
         nc.scalar.copy(out=table[:], in_=acc[3][1][:, 0:N_BITS])
 
-        gpsimd_bank(0)
+        gpsimd_piece(1, 0, 0)
         late = [regroup(nc.scalar.copy, x_raw[1][c], "byscalar", "gl%d" % c) for c in range(PASSES)]
 
         for h in range(N_TILE // FIRST_PIECE):
             spread(nc.vector, nc.sync, vfirst, acc[0][0], 0, 0, h, FIRST_PIECE)
         vector_spread(2, 0, 0)
         vector_spread(2, 0, 1)
+        vector_spread(1, 0, 1)
         for c in range(PASSES):
             quantise_x(late[c], c, 1)
             passes(c, 1)
+        gpsimd_piece(3, 1, 1)
         vector_spread(3, 0, 0)
         vector_spread(3, 0, 1)
-        for m in range(M_TILES):
+        for m in range(M_TILES - 1):
             vector_spread(m, 1, 0)
             vector_spread(m, 1, 1)
+        vector_spread(3, 1, 0)

@@ -22,6 +22,7 @@ N_TILES = IN_F // N_TILE
 PIECE = 256
 FIRST_PIECE = 128
 PAD_N = 32
+GPSIMD_PIECE = 192
 
 FLOPS = 2 * N_TOK * IN_F * OUT_F
 BYTES = 2 * N_TOK * (IN_F + OUT_F) + 2 * N_BITS + 4 * OUT_F * IN_F * N_BITS
@@ -83,17 +84,20 @@ def tile_auglag_kernel(tc, x, w_twos, b, base, grad_out, out):
             for m in range(M_TILES)
         ]
 
+        def one_pass(c, m, n):
+            nc.tensor.matmul_mx(
+                out=acc[m][n][:],
+                lhsT=g_codes[:, c, m * P : (m + 1) * P].bitcast(E5M2X4),
+                lhsT_scale=g_scales[:, c, m * P : (m + 1) * P],
+                rhs=x_codes[:, c, n * N_TILE : (n + 1) * N_TILE].bitcast(E4M3X4),
+                rhs_scale=x_scales[:, c, n * N_TILE : (n + 1) * N_TILE],
+                start=(c == 0),
+                stop=(c == PASSES - 1),
+            )
+
         def passes(c, n):
             for m in range(M_TILES):
-                nc.tensor.matmul_mx(
-                    out=acc[m][n][:],
-                    lhsT=g_codes[:, c, m * P : (m + 1) * P].bitcast(E5M2X4),
-                    lhsT_scale=g_scales[:, c, m * P : (m + 1) * P],
-                    rhs=x_codes[:, c, n * N_TILE : (n + 1) * N_TILE].bitcast(E4M3X4),
-                    rhs_scale=x_scales[:, c, n * N_TILE : (n + 1) * N_TILE],
-                    start=(c == 0),
-                    stop=(c == PASSES - 1),
-                )
+                one_pass(c, m, n)
 
         def spread(engine, queue, pool, sums, m, n, h, width=PIECE):
             t = pool.tile([P, width, N_BITS], F32, name="spread")
@@ -109,11 +113,12 @@ def tile_auglag_kernel(tc, x, w_twos, b, base, grad_out, out):
         def vector_spread(m, n, h):
             spread(nc.vector, nc.sync, vout, acc[m][n], m, n, h)
 
-        def gpsimd_piece(m, n, h):
+        def gpsimd_pieces(m, n, first, count, width):
             sums = gsum.tile([P, N_TILE], F32, name="sums")
-            cols = slice(h * PIECE, (h + 1) * PIECE)
+            cols = slice(first * width, (first + count) * width)
             nc.scalar.copy(out=sums[:, cols], in_=acc[m][n][:, cols])
-            spread(nc.gpsimd, nc.gpsimd, gout, sums, m, n, h)
+            for h in range(first, first + count):
+                spread(nc.gpsimd, nc.gpsimd, gout, sums, m, n, h, width)
 
         def quantise_x(grouped, c, n):
             cols = slice(n * N_TILE, (n + 1) * N_TILE)
@@ -129,21 +134,25 @@ def tile_auglag_kernel(tc, x, w_twos, b, base, grad_out, out):
                 nc.tensor.matmul(out=acc[3][1][:, 0:PAD_N], lhsT=step_mat[:], rhs=base_row[:], start=True, stop=True)
         nc.scalar.copy(out=table[:], in_=acc[3][1][:, 0:N_BITS])
 
-        gpsimd_piece(1, 0, 0)
+        gpsimd_pieces(1, 0, 0, 2, GPSIMD_PIECE)
         late = [regroup(nc.scalar.copy, x_raw[1][c], "byscalar", "gl%d" % c) for c in range(PASSES)]
 
         for h in range(N_TILE // FIRST_PIECE):
             spread(nc.vector, nc.sync, vfirst, acc[0][0], 0, 0, h, FIRST_PIECE)
         vector_spread(2, 0, 0)
         vector_spread(2, 0, 1)
-        vector_spread(1, 0, 1)
+        vector_spread(3, 0, 0)
+        spread(nc.vector, nc.sync, vfirst, acc[1][0], 1, 0, 3, FIRST_PIECE)
         for c in range(PASSES):
             quantise_x(late[c], c, 1)
-            passes(c, 1)
-        gpsimd_piece(3, 1, 1)
-        vector_spread(3, 0, 0)
+            one_pass(c, 0, 1)
+            one_pass(c, 1, 1)
+        for c in range(PASSES):
+            one_pass(c, 2, 1)
+            one_pass(c, 3, 1)
+        gpsimd_pieces(1, 1, 1, 1, PIECE)
         vector_spread(3, 0, 1)
-        for m in range(M_TILES - 1):
+        for m in range(M_TILES):
             vector_spread(m, 1, 0)
-            vector_spread(m, 1, 1)
-        vector_spread(3, 1, 0)
+            if m != 1:
+                vector_spread(m, 1, 1)

@@ -20,7 +20,8 @@ N_TILE = 512
 M_TILES = OUT_F // P
 N_TILES = IN_F // N_TILE
 PIECE = 256
-FIRST_PIECE = 128
+G_EARLY = 2 * P
+X_BY_VECTOR = 320
 PAD_N = 32
 GPSIMD_PIECE = 192
 
@@ -34,15 +35,18 @@ def tile_auglag_kernel(tc, x, w_twos, b, base, grad_out, out):
         raw = ctx.enter_context(tc.tile_pool(name="raw", bufs=1))
         keep = ctx.enter_context(tc.tile_pool(name="keep", bufs=1))
         grp = ctx.enter_context(tc.tile_pool(name="grp", bufs=4))
-        vout = ctx.enter_context(tc.tile_pool(name="vout", bufs=10))
-        gout = ctx.enter_context(tc.tile_pool(name="gout", bufs=2))
+        vout = ctx.enter_context(tc.tile_pool(name="vout", bufs=9))
+        gout = ctx.enter_context(tc.tile_pool(name="gout", bufs=3))
         gsum = ctx.enter_context(tc.tile_pool(name="gsum", bufs=2))
-        vfirst = ctx.enter_context(tc.tile_pool(name="vfirst", bufs=4))
+        vfirst = ctx.enter_context(tc.tile_pool(name="vfirst", bufs=8))
         psum = ctx.enter_context(tc.psum_pool(name="acc", bufs=1))
         ctx.enter_context(tc.manual_schedule())
 
-        g_codes = keep.tile([P, PASSES, OUT_F], U32, align_bytes=64)
-        g_scales = keep.tile([P, PASSES, OUT_F], U8, align_bytes=64)
+        g_codes = keep.tile([P, PASSES, G_EARLY], U32, align_bytes=64)
+        g_scales = keep.tile([P, PASSES, G_EARLY], U8, align_bytes=64)
+        h_codes = [keep.tile([P, PASSES * P], U32, name="h_codes%d" % m, align_bytes=64) for m in range(2)]
+        h_scales = [keep.tile([P, PASSES * P], U8, name="h_scales%d" % m, align_bytes=64) for m in range(2)]
+        h_grp = [keep.tile([P, PASSES * P, PACK], BF16, name="h_grp%d" % m, align_bytes=64) for m in range(2)]
         x_codes = keep.tile([P, PASSES, IN_F], U32, align_bytes=64)
         x_scales = keep.tile([P, PASSES, IN_F], U8, align_bytes=64)
         base_row = keep.tile([P, PAD_N], BF16)
@@ -58,25 +62,32 @@ def tile_auglag_kernel(tc, x, w_twos, b, base, grad_out, out):
             nc.sync.dma_start(out=t[:], in_=src.rearrange("(p j) w -> p j w", j=PACK))
             return t
 
-        g_raw = []
-        x_raw = [[], []]
-        for c in range(PASSES):
-            g_raw.append(load(grad_out[c * K_PASS : (c + 1) * K_PASS, :], "graw%d" % c))
-            x_raw[0].append(load(x[c * K_PASS : (c + 1) * K_PASS, 0:N_TILE], "xraw0%d" % c))
-        for c in range(PASSES):
-            x_raw[1].append(load(x[c * K_PASS : (c + 1) * K_PASS, N_TILE : 2 * N_TILE], "xraw1%d" % c))
+        g_raw = [None] * PASSES
+        x_raw = [[None] * PASSES, [None] * PASSES]
 
-        def regroup(copy, src, tag, name):
-            t = grp.tile([P, N_TILE, PACK], BF16, name=name, tag=tag, align_bytes=64)
-            copy(
-                out=t[:].rearrange("p (c i) t -> p c t i", i=4),
-                in_=src[:].rearrange("p t (c i) -> p c t i", i=4),
+        def load_g(c):
+            g_raw[c] = load(grad_out[c * K_PASS : (c + 1) * K_PASS, :], "graw%d" % c)
+
+        def load_x(c, n):
+            x_raw[n][c] = load(
+                x[c * K_PASS : (c + 1) * K_PASS, n * N_TILE : (n + 1) * N_TILE], "xraw%d%d" % (n, c)
             )
-            return t
+
+        for c in range(PASSES):
+            load_x(c, 0)
+            load_g(c)
+        for c in range(PASSES):
+            load_x(c, 1)
+
+        def regroup(copy, dst, src):
+            copy(
+                out=dst.rearrange("p (c i) t -> p c t i", i=4),
+                in_=src.rearrange("p t (c i) -> p c t i", i=4),
+            )
 
         def quantise(grouped, codes, scales, fmt):
             nc.vector.quantize_mx(
-                out=codes.bitcast(fmt), scales=scales, in_=grouped[:].rearrange("p w t -> p (w t)")
+                out=codes.bitcast(fmt), scales=scales, in_=grouped.rearrange("p w t -> p (w t)")
             )
 
         acc = [
@@ -85,64 +96,129 @@ def tile_auglag_kernel(tc, x, w_twos, b, base, grad_out, out):
         ]
 
         def one_pass(c, m, n):
+            if m < 2:
+                cols = slice(m * P, (m + 1) * P)
+                codes, scales = g_codes[:, c, cols], g_scales[:, c, cols]
+            else:
+                cols = slice(c * P, (c + 1) * P)
+                codes, scales = h_codes[m - 2][:, cols], h_scales[m - 2][:, cols]
             nc.tensor.matmul_mx(
                 out=acc[m][n][:],
-                lhsT=g_codes[:, c, m * P : (m + 1) * P].bitcast(E5M2X4),
-                lhsT_scale=g_scales[:, c, m * P : (m + 1) * P],
+                lhsT=codes.bitcast(E5M2X4),
+                lhsT_scale=scales,
                 rhs=x_codes[:, c, n * N_TILE : (n + 1) * N_TILE].bitcast(E4M3X4),
                 rhs_scale=x_scales[:, c, n * N_TILE : (n + 1) * N_TILE],
                 start=(c == 0),
                 stop=(c == PASSES - 1),
             )
 
-        def passes(c, n):
-            for m in range(M_TILES):
-                one_pass(c, m, n)
-
-        def spread(engine, queue, pool, sums, m, n, h, width=PIECE):
+        def spread(engine, pool, sums, m, n, first, width):
             t = pool.tile([P, width, N_BITS], F32, name="spread")
             engine.tensor_tensor(
                 out=t[:],
-                in0=sums[:, h * width : (h + 1) * width].unsqueeze(2).to_broadcast([P, width, N_BITS]),
+                in0=sums[:, first : first + width].unsqueeze(2).to_broadcast([P, width, N_BITS]),
                 in1=table[:].unsqueeze(1).to_broadcast([P, width, N_BITS]),
                 op=MULT,
             )
-            i0 = n * N_TILE + h * width
-            queue.dma_start(out=out[m * P : (m + 1) * P, i0 : i0 + width, :], in_=t[:])
+            i0 = n * N_TILE + first
+            return out[m * P : (m + 1) * P, i0 : i0 + width, :], t
+
+        def store(piece):
+            nc.sync.dma_start(out=piece[0], in_=piece[1][:])
+
+        def small_spread(m, n, first, width):
+            store(spread(nc.vector, vfirst, acc[m][n], m, n, first, width))
 
         def vector_spread(m, n, h):
-            spread(nc.vector, nc.sync, vout, acc[m][n], m, n, h)
+            store(spread(nc.vector, vout, acc[m][n], m, n, h * PIECE, PIECE))
 
-        def gpsimd_pieces(m, n, first, count, width):
+        def gpsimd_pieces(m, n, pieces):
             sums = gsum.tile([P, N_TILE], F32, name="sums")
-            cols = slice(first * width, (first + count) * width)
+            cols = slice(pieces[0][0], sum(pieces[-1]))
             nc.scalar.copy(out=sums[:, cols], in_=acc[m][n][:, cols])
-            for h in range(first, first + count):
-                spread(nc.gpsimd, nc.gpsimd, gout, sums, m, n, h, width)
+            return [spread(nc.gpsimd, gout, sums, m, n, first, width) for first, width in pieces]
 
         def quantise_x(grouped, c, n):
             cols = slice(n * N_TILE, (n + 1) * N_TILE)
-            quantise(grouped, x_codes[:, c, cols], x_scales[:, c, cols], E4M3X4)
+            quantise(grouped[:], x_codes[:, c, cols], x_scales[:, c, cols], E4M3X4)
 
+        def regroup_x(c):
+            cut = N_TILE if c == 0 else X_BY_VECTOR
+            t = grp.tile([P, N_TILE, PACK], BF16, name="gx%d" % c, tag="gx", align_bytes=64)
+            regroup(nc.vector.tensor_copy, t[:, 0:cut, :], x_raw[0][c][:, :, 0:cut])
+            if cut < N_TILE:
+                regroup(nc.scalar.copy, t[:, cut:N_TILE, :], x_raw[0][c][:, :, cut:N_TILE])
+            return t
+
+        def regroup_g(c):
+            t = grp.tile([P, G_EARLY, PACK], BF16, name="gg%d" % c, tag="gg", align_bytes=64)
+            if c < PASSES - 1:
+                regroup(nc.scalar.copy, t[:], g_raw[c][:, :, 0:G_EARLY])
+            else:
+                regroup(nc.vector.tensor_copy, t[:, 0:P, :], g_raw[c][:, :, 0:P])
+                regroup(nc.scalar.copy, t[:, P:G_EARLY, :], g_raw[c][:, :, P:G_EARLY])
+            return t
+
+        def finish_pass(c, gg):
+            quantise(gg[:], g_codes[:, c, :], g_scales[:, c, :], E5M2X4)
+            one_pass(c, 0, 0)
+            one_pass(c, 1, 0)
+
+        nc.tensor.matmul(out=acc[3][1][:, 0:PAD_N], lhsT=step_mat[:], rhs=base_row[:], start=True, stop=True)
+        gg = None
         for c in range(PASSES):
-            gg = regroup(nc.scalar.copy, g_raw[c], "byscalar", "gg%d" % c)
-            gx = regroup(nc.vector.tensor_copy, x_raw[0][c], "byvector", "gx%d" % c)
-            quantise(gg, g_codes[:, c, :], g_scales[:, c, :], E5M2X4)
+            gx = regroup_x(c)
+            if c > 0:
+                finish_pass(c - 1, gg)
             quantise_x(gx, c, 0)
-            passes(c, 0)
+            gg = regroup_g(c)
             if c == 1:
-                nc.tensor.matmul(out=acc[3][1][:, 0:PAD_N], lhsT=step_mat[:], rhs=base_row[:], start=True, stop=True)
-        nc.scalar.copy(out=table[:], in_=acc[3][1][:, 0:N_BITS])
+                nc.scalar.copy(out=table[:], in_=acc[3][1][:, 0:N_BITS])
+        finish_pass(PASSES - 1, gg)
 
-        gpsimd_pieces(1, 0, 0, 2, GPSIMD_PIECE)
-        late = [regroup(nc.scalar.copy, x_raw[1][c], "byscalar", "gl%d" % c) for c in range(PASSES)]
+        def regroup_h(m, c):
+            cols = slice(G_EARLY + m * P, G_EARLY + (m + 1) * P)
+            regroup(nc.scalar.copy, h_grp[m][:, c * P : (c + 1) * P, :], g_raw[c][:, :, cols])
 
-        for h in range(N_TILE // FIRST_PIECE):
-            spread(nc.vector, nc.sync, vfirst, acc[0][0], 0, 0, h, FIRST_PIECE)
-        vector_spread(2, 0, 0)
-        vector_spread(2, 0, 1)
+        late = []
+
+        def quantise_h(m):
+            quantise(h_grp[m - 2][:], h_codes[m - 2][:], h_scales[m - 2][:], E5M2X4)
+            for c in range(PASSES):
+                one_pass(c, m, 0)
+
+        def regroup_late(c):
+            t = grp.tile([P, N_TILE, PACK], BF16, name="gl%d" % c, tag="gx", align_bytes=64)
+            regroup(nc.scalar.copy, t[:], x_raw[1][c][:])
+            late.append(t)
+
+        regroup_h(0, 0)
+        regroup_h(0, 1)
+        early = gpsimd_pieces(1, 0, [(0, 192)])
+        regroup_h(0, 2)
+        regroup_h(0, 3)
+        for c in range(PASSES):
+            regroup_h(1, c)
+        small_spread(0, 0, 0, 64)
+        small_spread(0, 0, 64, 64)
+        for first in (128, 256, 384):
+            small_spread(0, 0, first, P)
+        small_spread(1, 0, 192, 128)
+        store(early[0])
+        quantise_h(2)
+        small_spread(1, 0, 320, 128)
+        quantise_h(3)
+        small_spread(1, 0, 448, 64)
+        regroup_late(0)
+        mid = gpsimd_pieces(2, 0, [(0, 192), (192, 128)])
+        regroup_late(1)
+        regroup_late(2)
+        regroup_late(3)
+        small_spread(2, 0, 320, 64)
+        small_spread(2, 0, 384, 128)
         vector_spread(3, 0, 0)
-        spread(nc.vector, nc.sync, vfirst, acc[1][0], 1, 0, 3, FIRST_PIECE)
+        vector_spread(3, 0, 1)
+        store(mid[0])
         for c in range(PASSES):
             quantise_x(late[c], c, 1)
             one_pass(c, 0, 1)
@@ -150,9 +226,14 @@ def tile_auglag_kernel(tc, x, w_twos, b, base, grad_out, out):
         for c in range(PASSES):
             one_pass(c, 2, 1)
             one_pass(c, 3, 1)
-        gpsimd_pieces(1, 1, 1, 1, PIECE)
-        vector_spread(3, 0, 1)
-        for m in range(M_TILES):
-            vector_spread(m, 1, 0)
-            if m != 1:
-                vector_spread(m, 1, 1)
+        store(mid[1])
+        last = gpsimd_pieces(1, 1, [(0, 192), (192, 192)])
+        vector_spread(0, 1, 0)
+        vector_spread(0, 1, 1)
+        small_spread(1, 1, 384, 128)
+        vector_spread(2, 1, 0)
+        store(last[0])
+        vector_spread(2, 1, 1)
+        vector_spread(3, 1, 0)
+        store(last[1])
+        vector_spread(3, 1, 1)

@@ -159,22 +159,29 @@ def tile_auglag_kernel(tc, x, w_twos, b, base, grad_out, out):
                 regroup(nc.scalar.copy, t[:, P:G_EARLY, :], g_raw[c][:, :, P:G_EARLY])
             return t
 
-        def finish_pass(c, gg):
-            quantise(gg[:], g_codes[:, c, :], g_scales[:, c, :], E5M2X4)
-            one_pass(c, 0, 0)
-            one_pass(c, 1, 0)
+        def quantise_g(c, gg, first, last):
+            cols = slice(first * P, last * P)
+            quantise(gg[:, cols, :], g_codes[:, c, cols], g_scales[:, c, cols], E5M2X4)
 
         nc.tensor.matmul(out=acc[3][1][:, 0:PAD_N], lhsT=step_mat[:], rhs=base_row[:], start=True, stop=True)
         gg = None
         for c in range(PASSES):
             gx = regroup_x(c)
             if c > 0:
-                finish_pass(c - 1, gg)
-            quantise_x(gx, c, 0)
-            gg = regroup_g(c)
+                quantise_g(c - 1, gg, 0, 2)
+                one_pass(c - 1, 0, 0)
+                one_pass(c - 1, 1, 0)
+            if c == PASSES - 1:
+                gg = regroup_g(c)
+                quantise_x(gx, c, 0)
+            else:
+                quantise_x(gx, c, 0)
+                gg = regroup_g(c)
             if c == 1:
                 nc.scalar.copy(out=table[:], in_=acc[3][1][:, 0:N_BITS])
-        finish_pass(PASSES - 1, gg)
+        for m in range(2):
+            quantise_g(PASSES - 1, gg, m, m + 1)
+            one_pass(PASSES - 1, m, 0)
 
         def regroup_h(m, c):
             cols = slice(G_EARLY + m * P, G_EARLY + (m + 1) * P)
@@ -194,39 +201,41 @@ def tile_auglag_kernel(tc, x, w_twos, b, base, grad_out, out):
 
         regroup_h(0, 0)
         regroup_h(0, 1)
-        early = gpsimd_pieces(1, 0, [(0, 192)])
         regroup_h(0, 2)
+        early = gpsimd_pieces(1, 0, [(0, 128)])
         regroup_h(0, 3)
         for c in range(PASSES):
             regroup_h(1, c)
-        small_spread(0, 0, 0, 64)
-        small_spread(0, 0, 64, 64)
-        for first in (128, 256, 384):
-            small_spread(0, 0, first, P)
-        small_spread(1, 0, 192, 128)
+        early += gpsimd_pieces(1, 0, [(128, 192)])
+        for first in (0, 64, 128, 192):
+            small_spread(0, 0, first, 64)
+        small_spread(0, 0, 256, P)
         store(early[0])
         quantise_h(2)
-        small_spread(1, 0, 320, 128)
         quantise_h(3)
+        small_spread(0, 0, 384, P)
+        small_spread(1, 0, 320, 128)
         small_spread(1, 0, 448, 64)
         regroup_late(0)
-        mid = gpsimd_pieces(2, 0, [(0, 192), (192, 128)])
+        mid = gpsimd_pieces(2, 0, [(0, 192)])
         regroup_late(1)
         regroup_late(2)
         regroup_late(3)
-        small_spread(2, 0, 320, 64)
+        small_spread(2, 0, 192, 64)
+        store(early[1])
+        small_spread(2, 0, 256, 128)
         small_spread(2, 0, 384, 128)
-        vector_spread(3, 0, 0)
-        vector_spread(3, 0, 1)
+        small_spread(3, 0, 0, 128)
+        small_spread(3, 0, 128, 128)
         store(mid[0])
         for c in range(PASSES):
             quantise_x(late[c], c, 1)
             one_pass(c, 0, 1)
-            one_pass(c, 1, 1)
-        for c in range(PASSES):
-            one_pass(c, 2, 1)
-            one_pass(c, 3, 1)
-        store(mid[1])
+        for m in (1, 2, 3):
+            for c in range(PASSES):
+                one_pass(c, m, 1)
+        small_spread(3, 0, 256, P)
+        small_spread(3, 0, 384, P)
         last = gpsimd_pieces(1, 1, [(0, 192), (192, 192)])
         vector_spread(0, 1, 0)
         vector_spread(0, 1, 1)

@@ -123,14 +123,14 @@ def tile_auglag_kernel(tc, x, w_twos, b, base, grad_out, out):
             i0 = n * N_TILE + first
             return out[m * P : (m + 1) * P, i0 : i0 + width, :], t
 
-        def store(piece):
-            nc.sync.dma_start(out=piece[0], in_=piece[1][:])
+        def store(piece, queue=nc.sync):
+            queue.dma_start(out=piece[0], in_=piece[1][:])
 
         def small_spread(m, n, first, width):
             store(spread(nc.vector, vfirst, acc[m][n], m, n, first, width))
 
-        def vector_spread(m, n, h):
-            store(spread(nc.vector, vout, acc[m][n], m, n, h * PIECE, PIECE))
+        def vector_spread(m, n, h, queue=nc.sync):
+            store(spread(nc.vector, vout, acc[m][n], m, n, h * PIECE, PIECE), queue)
 
         def gpsimd_pieces(m, n, pieces):
             sums = gsum.tile([P, N_TILE], F32, name="sums")
@@ -238,11 +238,11 @@ def tile_auglag_kernel(tc, x, w_twos, b, base, grad_out, out):
         small_spread(3, 0, 384, P)
         last = gpsimd_pieces(1, 1, [(0, 192), (192, 192)])
         vector_spread(0, 1, 0)
-        vector_spread(0, 1, 1)
+        vector_spread(0, 1, 1, nc.scalar)
         small_spread(1, 1, 384, 128)
-        vector_spread(2, 1, 0)
+        vector_spread(2, 1, 0, nc.scalar)
         store(last[0])
-        vector_spread(2, 1, 1)
+        vector_spread(2, 1, 1, nc.scalar)
         vector_spread(3, 1, 0)
-        store(last[1])
+        store(last[1], nc.scalar)
         vector_spread(3, 1, 1)

@@ -36,9 +36,9 @@ def tile_auglag_kernel(tc, x, w_twos, b, base, grad_out, out):
         keep = ctx.enter_context(tc.tile_pool(name="keep", bufs=1))
         grp = ctx.enter_context(tc.tile_pool(name="grp", bufs=4))
         vout = ctx.enter_context(tc.tile_pool(name="vout", bufs=9))
-        gout = ctx.enter_context(tc.tile_pool(name="gout", bufs=3))
+        gout = ctx.enter_context(tc.tile_pool(name="gout", bufs=2))
         gsum = ctx.enter_context(tc.tile_pool(name="gsum", bufs=2))
-        vfirst = ctx.enter_context(tc.tile_pool(name="vfirst", bufs=8))
+        vfirst = ctx.enter_context(tc.tile_pool(name="vfirst", bufs=6))
         psum = ctx.enter_context(tc.psum_pool(name="acc", bufs=1))
         ctx.enter_context(tc.manual_schedule())
 
@@ -126,11 +126,9 @@ def tile_auglag_kernel(tc, x, w_twos, b, base, grad_out, out):
         def store(piece, queue=nc.sync):
             queue.dma_start(out=piece[0], in_=piece[1][:])
 
-        def small_spread(m, n, first, width):
-            store(spread(nc.vector, vfirst, acc[m][n], m, n, first, width))
-
-        def vector_spread(m, n, h, queue=nc.sync):
-            store(spread(nc.vector, vout, acc[m][n], m, n, h * PIECE, PIECE), queue)
+        def vector_piece(m, n, first, width, queue=nc.sync):
+            pool = vfirst if width <= P else vout
+            store(spread(nc.vector, pool, acc[m][n], m, n, first, width), queue)
 
         def gpsimd_pieces(m, n, pieces):
             sums = gsum.tile([P, N_TILE], F32, name="sums")
@@ -163,6 +161,14 @@ def tile_auglag_kernel(tc, x, w_twos, b, base, grad_out, out):
             cols = slice(first * P, last * P)
             quantise(gg[:, cols, :], g_codes[:, c, cols], g_scales[:, c, cols], E5M2X4)
 
+        def regroup_h(copy, m, c):
+            cols = slice(G_EARLY + m * P, G_EARLY + (m + 1) * P)
+            regroup(copy, h_grp[m][:, c * P : (c + 1) * P, :], g_raw[c][:, :, cols])
+
+        def quantise_h(m, first, last):
+            cols = slice(first * P, last * P)
+            quantise(h_grp[m - 2][:, cols, :], h_codes[m - 2][:, cols], h_scales[m - 2][:, cols], E5M2X4)
+
         nc.tensor.matmul(out=acc[3][1][:, 0:PAD_N], lhsT=step_mat[:], rhs=base_row[:], start=True, stop=True)
         gg = None
         for c in range(PASSES):
@@ -177,56 +183,49 @@ def tile_auglag_kernel(tc, x, w_twos, b, base, grad_out, out):
             else:
                 quantise_x(gx, c, 0)
                 gg = regroup_g(c)
+                regroup_h(nc.vector.tensor_copy, 0, c)
+                if c > 0:
+                    quantise_h(2, c - 1, c)
             if c == 1:
                 nc.scalar.copy(out=table[:], in_=acc[3][1][:, 0:N_BITS])
         for m in range(2):
             quantise_g(PASSES - 1, gg, m, m + 1)
             one_pass(PASSES - 1, m, 0)
 
-        def regroup_h(m, c):
-            cols = slice(G_EARLY + m * P, G_EARLY + (m + 1) * P)
-            regroup(nc.scalar.copy, h_grp[m][:, c * P : (c + 1) * P, :], g_raw[c][:, :, cols])
-
         late = []
-
-        def quantise_h(m):
-            quantise(h_grp[m - 2][:], h_codes[m - 2][:], h_scales[m - 2][:], E5M2X4)
-            for c in range(PASSES):
-                one_pass(c, m, 0)
 
         def regroup_late(c):
             t = grp.tile([P, N_TILE, PACK], BF16, name="gl%d" % c, tag="gx", align_bytes=64)
             regroup(nc.scalar.copy, t[:], x_raw[1][c][:])
             late.append(t)
 
-        regroup_h(0, 0)
-        regroup_h(0, 1)
-        regroup_h(0, 2)
+        regroup_h(nc.scalar.copy, 0, 3)
+        regroup_h(nc.scalar.copy, 1, 0)
+        regroup_h(nc.scalar.copy, 1, 1)
         early = gpsimd_pieces(1, 0, [(0, 128)])
-        regroup_h(0, 3)
-        for c in range(PASSES):
-            regroup_h(1, c)
-        early += gpsimd_pieces(1, 0, [(128, 192)])
-        for first in (0, 64, 128, 192):
-            small_spread(0, 0, first, 64)
-        small_spread(0, 0, 256, P)
+        regroup_h(nc.scalar.copy, 1, 2)
+        regroup_h(nc.scalar.copy, 1, 3)
+        vector_piece(0, 0, 0, 64)
+        vector_piece(0, 0, 64, 64)
+        vector_piece(0, 0, 128, 128)
         store(early[0])
-        quantise_h(2)
-        quantise_h(3)
-        small_spread(0, 0, 384, P)
-        small_spread(1, 0, 320, 128)
-        small_spread(1, 0, 448, 64)
+        vector_piece(0, 0, 256, 256)
+        quantise_h(2, 2, 4)
+        quantise_h(3, 0, 4)
+        for m in (2, 3):
+            for c in range(PASSES):
+                one_pass(c, m, 0)
+        vector_piece(1, 0, 320, 192)
         regroup_late(0)
-        mid = gpsimd_pieces(2, 0, [(0, 192)])
+        early += gpsimd_pieces(1, 0, [(128, 192)])
         regroup_late(1)
+        mid = gpsimd_pieces(2, 0, [(0, 128)])
         regroup_late(2)
         regroup_late(3)
-        small_spread(2, 0, 192, 64)
+        vector_piece(2, 0, 128, 128)
         store(early[1])
-        small_spread(2, 0, 256, 128)
-        small_spread(2, 0, 384, 128)
-        small_spread(3, 0, 0, 128)
-        small_spread(3, 0, 128, 128)
+        vector_piece(2, 0, 256, 256)
+        vector_piece(3, 0, 0, 256)
         store(mid[0])
         for c in range(PASSES):
             quantise_x(late[c], c, 1)
@@ -234,15 +233,13 @@ def tile_auglag_kernel(tc, x, w_twos, b, base, grad_out, out):
         for m in (1, 2, 3):
             for c in range(PASSES):
                 one_pass(c, m, 1)
-        small_spread(3, 0, 256, P)
-        small_spread(3, 0, 384, P)
-        last = gpsimd_pieces(1, 1, [(0, 192), (192, 192)])
-        vector_spread(0, 1, 0)
-        vector_spread(0, 1, 1, nc.scalar)
-        small_spread(1, 1, 384, 128)
-        vector_spread(2, 1, 0, nc.scalar)
+        vector_piece(3, 0, 256, 256)
+        last = gpsimd_pieces(1, 1, [(256, 256)])
+        vector_piece(0, 1, 0, 256)
+        vector_piece(0, 1, 256, 256, nc.scalar)
+        vector_piece(1, 1, 0, 256)
+        vector_piece(2, 1, 0, 256, nc.scalar)
         store(last[0])
-        vector_spread(2, 1, 1, nc.scalar)
-        vector_spread(3, 1, 0)
-        store(last[1], nc.scalar)
-        vector_spread(3, 1, 1)
+        vector_piece(2, 1, 256, 256, nc.scalar)
+        vector_piece(3, 1, 0, 256)
+        vector_piece(3, 1, 256, 256)

@@ -191,37 +191,41 @@ def tile_auglag_kernel(tc, x, w_twos, b, base, grad_out, out):
         for m in range(2):
             quantise_g(PASSES - 1, gg, m, m + 1)
             one_pass(PASSES - 1, m, 0)
+        regroup_h(nc.vector.tensor_copy, 0, PASSES - 1)
+        for c in (PASSES - 2, PASSES - 1):
+            quantise_h(2, c, c + 1)
+        for c in range(PASSES):
+            one_pass(c, 2, 0)
 
         late = []
 
-        def regroup_late(c):
-            t = grp.tile([P, N_TILE, PACK], BF16, name="gl%d" % c, tag="gx", align_bytes=64)
-            regroup(nc.scalar.copy, t[:], x_raw[1][c][:])
-            late.append(t)
+        def regroup_late(c, first, last):
+            if first == 0:
+                late.append(grp.tile([P, N_TILE, PACK], BF16, name="gl%d" % c, tag="gx", align_bytes=64))
+            regroup(nc.scalar.copy, late[c][:, first:last, :], x_raw[1][c][:, :, first:last])
 
-        regroup_h(nc.scalar.copy, 0, 3)
         regroup_h(nc.scalar.copy, 1, 0)
         regroup_h(nc.scalar.copy, 1, 1)
-        early = gpsimd_pieces(1, 0, [(0, 128)])
         regroup_h(nc.scalar.copy, 1, 2)
+        early = gpsimd_pieces(1, 0, [(0, 128)])
         regroup_h(nc.scalar.copy, 1, 3)
         vector_piece(0, 0, 0, 64)
         vector_piece(0, 0, 64, 64)
         vector_piece(0, 0, 128, 128)
+        vector_piece(0, 0, 256, 128)
         store(early[0])
-        vector_piece(0, 0, 256, 256)
-        quantise_h(2, 2, 4)
-        quantise_h(3, 0, 4)
-        for m in (2, 3):
-            for c in range(PASSES):
-                one_pass(c, m, 0)
-        vector_piece(1, 0, 320, 192)
-        regroup_late(0)
+        quantise_h(3, 0, PASSES)
+        for c in range(PASSES):
+            one_pass(c, 3, 0)
+        regroup_late(0, 0, N_TILE)
+        regroup_late(1, 0, PIECE)
         early += gpsimd_pieces(1, 0, [(128, 192)])
-        regroup_late(1)
+        regroup_late(1, PIECE, N_TILE)
+        vector_piece(0, 0, 384, 128)
+        vector_piece(1, 0, 320, 192)
         mid = gpsimd_pieces(2, 0, [(0, 128)])
-        regroup_late(2)
-        regroup_late(3)
+        regroup_late(2, 0, N_TILE)
+        regroup_late(3, 0, N_TILE)
         vector_piece(2, 0, 128, 128)
         store(early[1])
         vector_piece(2, 0, 256, 256)

@@ -238,12 +238,11 @@ def tile_auglag_kernel(tc, x, w_twos, b, base, grad_out, out):
             for c in range(PASSES):
                 one_pass(c, m, 1)
         vector_piece(3, 0, 256, 256)
-        last = gpsimd_pieces(1, 1, [(256, 256)])
         vector_piece(0, 1, 0, 256)
         vector_piece(0, 1, 256, 256, nc.scalar)
         vector_piece(1, 1, 0, 256)
-        vector_piece(2, 1, 0, 256, nc.scalar)
-        store(last[0])
+        vector_piece(1, 1, 256, 256, nc.scalar)
+        vector_piece(2, 1, 0, 256)
         vector_piece(2, 1, 256, 256, nc.scalar)
         vector_piece(3, 1, 0, 256)
         vector_piece(3, 1, 256, 256)

from contextlib import ExitStack

import concourse.mybir as mybir

F32 = mybir.dt.float32
BF16 = mybir.dt.bfloat16
U32 = mybir.dt.uint32
U8 = mybir.dt.uint8
E4M3X4 = mybir.dt.float8_e4m3fn_x4
E5M2X4 = mybir.dt.float8_e5m2_x4
MULT = mybir.AluOpType.mult

P = 128
PACK = 4
K_PASS = P * PACK
N_TOK, IN_F, OUT_F, N_BITS = 2048, 1024, 512, 8
STEP_SIZE = 0.0078125
PASSES = N_TOK // K_PASS
N_TILE = 512
M_TILES = OUT_F // P
N_TILES = IN_F // N_TILE
PIECE = 256
G_EARLY = 2 * P
X_BY_VECTOR = 320
PAD_N = 32
GPSIMD_PIECE = 192

FLOPS = 2 * N_TOK * IN_F * OUT_F
BYTES = 2 * N_TOK * (IN_F + OUT_F) + 2 * N_BITS + 4 * OUT_F * IN_F * N_BITS


def tile_auglag_kernel(tc, x, w_twos, b, base, grad_out, out):
    nc = tc.nc
    with ExitStack() as ctx:
        raw = ctx.enter_context(tc.tile_pool(name="raw", bufs=1))
        keep = ctx.enter_context(tc.tile_pool(name="keep", bufs=1))
        grp = ctx.enter_context(tc.tile_pool(name="grp", bufs=4))
        vout = ctx.enter_context(tc.tile_pool(name="vout", bufs=9))
        gout = ctx.enter_context(tc.tile_pool(name="gout", bufs=2))
        gsum = ctx.enter_context(tc.tile_pool(name="gsum", bufs=2))
        vfirst = ctx.enter_context(tc.tile_pool(name="vfirst", bufs=6))
        psum = ctx.enter_context(tc.psum_pool(name="acc", bufs=1))
        ctx.enter_context(tc.manual_schedule())

        g_codes = keep.tile([P, PASSES, G_EARLY], U32, align_bytes=64)
        g_scales = keep.tile([P, PASSES, G_EARLY], U8, align_bytes=64)
        h_codes = [keep.tile([P, PASSES * P], U32, name="h_codes%d" % m, align_bytes=64) for m in range(2)]
        h_scales = [keep.tile([P, PASSES * P], U8, name="h_scales%d" % m, align_bytes=64) for m in range(2)]
        h_grp = [keep.tile([P, PASSES * P, PACK], BF16, name="h_grp%d" % m, align_bytes=64) for m in range(2)]
        x_codes = keep.tile([P, PASSES, IN_F], U32, align_bytes=64)
        x_scales = keep.tile([P, PASSES, IN_F], U8, align_bytes=64)
        base_row = keep.tile([P, PAD_N], BF16)
        step_mat = keep.tile([P, P], BF16)
        table = keep.tile([P, N_BITS], F32)

        nc.vector.memset(base_row[:], 0.0)
        nc.gpsimd.memset(step_mat[:], STEP_SIZE)
        nc.scalar.dma_start(out=base_row[0:1, 0:N_BITS], in_=base.rearrange("a b k -> (a b) k"))

        def load(src, name):
            t = raw.tile([P, PACK, N_TILE], BF16, name=name)
            nc.sync.dma_start(out=t[:], in_=src.rearrange("(p j) w -> p j w", j=PACK))
            return t

        g_raw = [None] * PASSES
        x_raw = [[None] * PASSES, [None] * PASSES]

        def load_g(c):
            g_raw[c] = load(grad_out[c * K_PASS : (c + 1) * K_PASS, :], "graw%d" % c)

        def load_x(c, n):
            x_raw[n][c] = load(
                x[c * K_PASS : (c + 1) * K_PASS, n * N_TILE : (n + 1) * N_TILE], "xraw%d%d" % (n, c)
            )

        for c in range(PASSES):
            load_x(c, 0)
            load_g(c)
        for c in range(PASSES):
            load_x(c, 1)

        def regroup(copy, dst, src):
            copy(
                out=dst.rearrange("p (c i) t -> p c t i", i=4),
                in_=src.rearrange("p t (c i) -> p c t i", i=4),
            )

        def quantise(grouped, codes, scales, fmt):
            nc.vector.quantize_mx(
                out=codes.bitcast(fmt), scales=scales, in_=grouped.rearrange("p w t -> p (w t)")
            )

        acc = [
            [psum.tile([P, N_TILE], F32, name="acc%d%d" % (m, n)) for n in range(N_TILES)]
            for m in range(M_TILES)
        ]

        def one_pass(c, m, n):
            if m < 2:
                cols = slice(m * P, (m + 1) * P)
                codes, scales = g_codes[:, c, cols], g_scales[:, c, cols]
            else:
                cols = slice(c * P, (c + 1) * P)
                codes, scales = h_codes[m - 2][:, cols], h_scales[m - 2][:, cols]
            nc.tensor.matmul_mx(
                out=acc[m][n][:],
                lhsT=codes.bitcast(E5M2X4),
                lhsT_scale=scales,
                rhs=x_codes[:, c, n * N_TILE : (n + 1) * N_TILE].bitcast(E4M3X4),
                rhs_scale=x_scales[:, c, n * N_TILE : (n + 1) * N_TILE],
                start=(c == 0),
                stop=(c == PASSES - 1),
            )

        def spread(engine, pool, sums, m, n, first, width):
            t = pool.tile([P, width, N_BITS], F32, name="spread")
            engine.tensor_tensor(
                out=t[:],
                in0=sums[:, first : first + width].unsqueeze(2).to_broadcast([P, width, N_BITS]),
                in1=table[:].unsqueeze(1).to_broadcast([P, width, N_BITS]),
                op=MULT,
            )
            i0 = n * N_TILE + first
            return out[m * P : (m + 1) * P, i0 : i0 + width, :], t

        def store(piece, queue=nc.sync):
            queue.dma_start(out=piece[0], in_=piece[1][:])

        def vector_piece(m, n, first, width, queue=nc.sync):
            pool = vfirst if width <= P else vout
            store(spread(nc.vector, pool, acc[m][n], m, n, first, width), queue)

        def gpsimd_pieces(m, n, pieces):
            sums = gsum.tile([P, N_TILE], F32, name="sums")
            cols = slice(pieces[0][0], sum(pieces[-1]))
            nc.scalar.copy(out=sums[:, cols], in_=acc[m][n][:, cols])
            return [spread(nc.gpsimd, gout, sums, m, n, first, width) for first, width in pieces]

        def quantise_x(grouped, c, n):
            cols = slice(n * N_TILE, (n + 1) * N_TILE)
            quantise(grouped[:], x_codes[:, c, cols], x_scales[:, c, cols], E4M3X4)

        def regroup_x(c):
            cut = N_TILE if c == 0 else X_BY_VECTOR
            t = grp.tile([P, N_TILE, PACK], BF16, name="gx%d" % c, tag="gx", align_bytes=64)
            regroup(nc.vector.tensor_copy, t[:, 0:cut, :], x_raw[0][c][:, :, 0:cut])
            if cut < N_TILE:
                regroup(nc.scalar.copy, t[:, cut:N_TILE, :], x_raw[0][c][:, :, cut:N_TILE])
            return t

        def regroup_g(c):
            t = grp.tile([P, G_EARLY, PACK], BF16, name="gg%d" % c, tag="gg", align_bytes=64)
            if c < PASSES - 1:
                regroup(nc.scalar.copy, t[:], g_raw[c][:, :, 0:G_EARLY])
            else:
                regroup(nc.vector.tensor_copy, t[:, 0:P, :], g_raw[c][:, :, 0:P])
                regroup(nc.scalar.copy, t[:, P:G_EARLY, :], g_raw[c][:, :, P:G_EARLY])
            return t

        def quantise_g(c, gg, first, last):
            cols = slice(first * P, last * P)
            quantise(gg[:, cols, :], g_codes[:, c, cols], g_scales[:, c, cols], E5M2X4)

        def regroup_h(copy, m, c):
            cols = slice(G_EARLY + m * P, G_EARLY + (m + 1) * P)
            regroup(copy, h_grp[m][:, c * P : (c + 1) * P, :], g_raw[c][:, :, cols])

        def quantise_h(m, first, last):
            cols = slice(first * P, last * P)
            quantise(h_grp[m - 2][:, cols, :], h_codes[m - 2][:, cols], h_scales[m - 2][:, cols], E5M2X4)

        nc.tensor.matmul(out=acc[3][1][:, 0:PAD_N], lhsT=step_mat[:], rhs=base_row[:], start=True, stop=True)
        gg = None
        for c in range(PASSES):
            gx = regroup_x(c)
            if c > 0:
                quantise_g(c - 1, gg, 0, 2)
                one_pass(c - 1, 0, 0)
                one_pass(c - 1, 1, 0)
            if c == PASSES - 1:
                gg = regroup_g(c)
                quantise_x(gx, c, 0)
            else:
                quantise_x(gx, c, 0)
                gg = regroup_g(c)
                regroup_h(nc.vector.tensor_copy, 0, c)
                if c > 0:
                    quantise_h(2, c - 1, c)
            if c == 1:
                nc.scalar.copy(out=table[:], in_=acc[3][1][:, 0:N_BITS])
        for m in range(2):
            quantise_g(PASSES - 1, gg, m, m + 1)
            one_pass(PASSES - 1, m, 0)
        regroup_h(nc.vector.tensor_copy, 0, PASSES - 1)
        for c in (PASSES - 2, PASSES - 1):
            quantise_h(2, c, c + 1)
        for c in range(PASSES):
            one_pass(c, 2, 0)

        late = []

        def regroup_late(c, first, last):
            if first == 0:
                late.append(grp.tile([P, N_TILE, PACK], BF16, name="gl%d" % c, tag="gx", align_bytes=64))
            regroup(nc.scalar.copy, late[c][:, first:last, :], x_raw[1][c][:, :, first:last])

        regroup_h(nc.scalar.copy, 1, 0)
        regroup_h(nc.scalar.copy, 1, 1)
        regroup_h(nc.scalar.copy, 1, 2)
        early = gpsimd_pieces(1, 0, [(0, 128)])
        regroup_h(nc.scalar.copy, 1, 3)
        vector_piece(0, 0, 0, 64)
        vector_piece(0, 0, 64, 64)
        vector_piece(0, 0, 128, 128)
        vector_piece(0, 0, 256, 128)
        store(early[0])
        quantise_h(3, 0, PASSES)
        for c in range(PASSES):
            one_pass(c, 3, 0)
        regroup_late(0, 0, N_TILE)
        regroup_late(1, 0, PIECE)
        early += gpsimd_pieces(1, 0, [(128, 192)])
        regroup_late(1, PIECE, N_TILE)
        vector_piece(0, 0, 384, 128)
        vector_piece(1, 0, 320, 192)
        mid = gpsimd_pieces(2, 0, [(0, 128)])
        regroup_late(2, 0, N_TILE)
        regroup_late(3, 0, N_TILE)
        vector_piece(2, 0, 128, 128)
        store(early[1])
        vector_piece(2, 0, 256, 256)
        vector_piece(3, 0, 0, 256)
        store(mid[0])
        for c in range(PASSES):
            quantise_x(late[c], c, 1)
            one_pass(c, 0, 1)
        for m in (1, 2, 3):
            for c in range(PASSES):
                one_pass(c, m, 1)
        vector_piece(3, 0, 256, 256)
        vector_piece(0, 1, 0, 256)
        vector_piece(0, 1, 256, 256, nc.scalar)
        vector_piece(1, 1, 0, 256)
        vector_piece(1, 1, 256, 256, nc.scalar)
        vector_piece(2, 1, 0, 256)
        vector_piece(2, 1, 256, 256, nc.scalar)
        vector_piece(3, 1, 0, 256)
        vector_piece(3, 1, 256, 256)
